import numpy as np
import ml_dtypes


def mxq(x, axis, fmt="e4m3"):
    dtype, down = {"e4m3": (ml_dtypes.float8_e4m3fn, 7), "e5m2": (ml_dtypes.float8_e5m2, 14)}[fmt]
    v = np.moveaxis(np.asarray(x, np.float32).astype(ml_dtypes.bfloat16).astype(np.float64), axis, -1)
    blocks = v.reshape(v.shape[:-1] + (-1, 32))
    amax = np.abs(blocks).max(-1, keepdims=True)
    byte = np.maximum(np.where(amax > 0, np.frexp(amax)[1] - 1 + 127, 0) - down, 1)
    scale = np.exp2(byte - 127.0)
    codes = (blocks / scale).astype(np.float32).astype(dtype).astype(np.float64)
    return np.moveaxis((codes * scale).reshape(v.shape), -1, axis)


WIDE = False


def mx_kscale(k):
    if not WIDE:
        return np.ones(k)
    levels = np.array([10, -10, 5, -5, 0])
    a = np.random.permutation(np.resize(levels, k // 512 * 4)).reshape(k // 512, 4)
    idx = np.arange(k)
    return np.exp2(a[idx // 512, idx % 128 // 32])


BF16 = ml_dtypes.bfloat16


def bf(x):
    return np.asarray(x, np.float32).astype(BF16)


def f64(x):
    return np.asarray(x).astype(np.float64)


N, M, D = 8192, 512, 256
TEMPS = (0.02, 0.05, 0.2)
NT = len(TEMPS)
R = 1.5
SIG = R / np.sqrt(2.0 * D)


def drift_size(keys):
    s = SIG / np.asarray(TEMPS)
    return SIG * np.sqrt(np.minimum(np.exp(0.75 * s * s) / keys, 0.04) + s * s / (2.0 * D))


def setup_inputs():
    s = mx_kscale(M)
    w = s / s.min()
    near = (w < 2.0).sum()
    return {"gen_features": bf(np.random.standard_normal((N, D)) * SIG),
            "pos_features": bf(np.random.standard_normal((M, D)) * SIG * w[:, None]),
            "drift_scales": bf(drift_size(near) * (1.0 + 0.1 * np.random.standard_normal(NT)))}


def reference(gen_features, pos_features, drift_scales):
    gen, pos, sc = f64(gen_features), f64(pos_features), f64(drift_scales)
    dsq = (gen * gen).sum(-1)[:, None] + (pos * pos).sum(-1)[None, :] - 2.0 * (gen @ pos.T)
    d_att = np.sqrt(np.maximum(dsq, 0.0))
    posq = mxq(pos, 0, "e4m3")
    out = np.zeros_like(gen)
    for i, T in enumerate(TEMPS):
        logits = -d_att / T
        e = np.exp(logits - logits.max(1, keepdims=True))
        out = out + (mxq(e, 1, "e4m3") @ posq) / e.sum(1, keepdims=True) / sc[i]
    return out

@@ -1,0 +1,345 @@
+from contextlib import ExitStack
+
+import concourse.mybir as mybir
+from concourse.masks import make_identity
+
+F32 = mybir.dt.float32
+BF16 = mybir.dt.bfloat16
+U32 = mybir.dt.uint32
+U8 = mybir.dt.uint8
+FP8X4 = mybir.dt.float8_e4m3fn_x4
+FUNC = mybir.ActivationFunctionType
+ALU = mybir.AluOpType
+
+P = 128
+N_GEN = 8192
+N_POS = 512
+DIM = 256
+TEMPS = (0.02, 0.05, 0.2)
+N_T = len(TEMPS)
+
+TILES = N_GEN // P
+PAIR = 2
+STEPS = TILES // PAIR
+POS_TILES = N_POS // P
+WORDS = DIM // 2
+HALVES = 2
+PACK = 4
+
+BATCH = 8
+AHEAD = BATCH + 3
+E_BUFS = 5
+
+FLOPS = 2 * N_GEN * N_POS * DIM * (1 + N_T)
+
+
+def tile_driftingfield_pa_t_kernel(tc, gen_features, pos_features, drift_scales, out):
+    nc = tc.nc
+    gen_rows = gen_features.rearrange("(p t) d -> p (t d)", t=TILES)
+    out_rows = out.rearrange("(p t) d -> p (t d)", t=TILES)
+
+    with ExitStack() as ctx:
+        ctx.enter_context(tc.manual_schedule())
+        const = ctx.enter_context(tc.tile_pool(name="const", bufs=1))
+        junk_pool = ctx.enter_context(tc.tile_pool(name="junk", bufs=4))
+        gen_t_pool = ctx.enter_context(tc.tile_pool(name="gen_t", bufs=3))
+        dist_pool = ctx.enter_context(tc.tile_pool(name="dist", bufs=AHEAD + 1))
+        e_pool = ctx.enter_context(tc.tile_pool(name="e", bufs=E_BUFS))
+        mx_pool = ctx.enter_context(tc.tile_pool(name="mx", bufs=N_T))
+        res_pool = ctx.enter_context(tc.tile_pool(name="res", bufs=3))
+        psum_v = ctx.enter_context(tc.psum_pool(name="psum_v", bufs=2))
+        psum_g = ctx.enter_context(tc.psum_pool(name="psum_g", bufs=1))
+        psum_turn = ctx.enter_context(tc.psum_pool(name="psum_turn", bufs=2))
+        psum_o = ctx.enter_context(tc.psum_pool(name="psum_o", bufs=N_T))
+
+        pos_rows = const.tile([P, POS_TILES * DIM], BF16)
+        nc.sync.dma_start(
+            out=pos_rows[:].rearrange("p (b d) -> p b d", b=POS_TILES),
+            in_=pos_features.rearrange("(b p) d -> p b d", p=P),
+        )
+        gen_sb = const.tile([P, TILES * DIM], BF16)
+        load_cols = 8 * DIM
+        nc.sync.dma_start(out=gen_sb[:, 0:load_cols], in_=gen_rows[:, 0:load_cols])
+        pos_k = const.tile([P, PACK * DIM], BF16)
+        nc.sync.dma_start(
+            out=pos_k[:].rearrange("w (u r) -> w u r", u=2),
+            in_=pos_features.rearrange("(u w h) c -> w u (h c)", u=2, h=HALVES),
+        )
+        scale_bf = const.tile([P, N_T], BF16)
+        nc.sync.dma_start(out=scale_bf[:], in_=drift_scales.partition_broadcast(P))
+        for c0 in range(load_cols, TILES * DIM, load_cols):
+            nc.sync.dma_start(out=gen_sb[:, c0 : c0 + load_cols], in_=gen_rows[:, c0 : c0 + load_cols])
+        gen_words = gen_sb[:].bitcast(F32)
+
+        ident = const.tile([P, P], F32)
+        make_identity(nc, ident[:])
+
+        warm = const.tile([P, 1], F32)
+        nc.vector.memset(warm[:], 1.0)
+        nc.scalar.activation(out=warm[:], in_=warm[:], func=FUNC.Sqrt)
+
+        gen_sq = const.tile([P, TILES], F32)
+        v_max = const.tile([P, TILES], F32)
+        s_min = const.tile([P, TILES], F32)
+        d_min = const.tile([P, TILES], F32)
+        shift = const.tile([P, N_T * TILES], F32)
+        row_sum = const.tile([P, TILES * N_T], F32)
+        denom = const.tile([P, TILES * N_T], F32)
+        weight = const.tile([P, TILES * N_T], F32)
+
+        pos_sq = const.tile([P, POS_TILES], F32)
+        for b in range(POS_TILES):
+            squares = junk_pool.tile([P, DIM], BF16)
+            nc.scalar.activation(
+                out=squares[:],
+                in_=pos_rows[:, b * DIM : (b + 1) * DIM],
+                func=FUNC.Square,
+                accum_out=pos_sq[:, b : b + 1],
+            )
+        neg_pos_sq = const.tile([P, POS_TILES * P], F32)
+        nc.vector.tensor_scalar(
+            out=neg_pos_sq[:].rearrange("p (b c) -> p b c", b=POS_TILES),
+            in0=pos_sq[:].unsqueeze(2).to_broadcast([P, POS_TILES, P]),
+            scalar1=-1.0,
+            scalar2=None,
+            op0=ALU.mult,
+        )
+
+        pos_words = pos_rows[:].bitcast(F32)
+        pos_turned = psum_turn.tile([P, POS_TILES * P], F32, tag="turned")
+        for b in range(POS_TILES):
+            nc.tensor.transpose(
+                pos_turned[:, b * P : (b + 1) * P], pos_words[:, b * WORDS : (b + 1) * WORDS], ident[:]
+            )
+        pos2_t = const.tile([P, HALVES * N_POS], BF16)
+        nc.vector.tensor_scalar(
+            out=pos2_t[:].rearrange("w (h j) -> w h j", h=HALVES),
+            in0=pos_turned[:].bitcast(BF16).rearrange("w (j h) -> w h j", h=HALVES),
+            scalar1=2.0,
+            scalar2=None,
+            op0=ALU.mult,
+        )
+
+        drift = const.tile([P, N_T], F32)
+        nc.vector.tensor_copy(out=drift[:], in_=scale_bf[:])
+
+        gen_t_of = {}
+        dist_of = {}
+        e_of = {}
+        grouped_of = {}
+        codes_of = {}
+        scales_of = {}
+        prod_of = {}
+
+        def norms(k):
+            for a in range(PAIR):
+                i = k * PAIR + a
+                squares = junk_pool.tile([P, DIM], BF16)
+                nc.scalar.activation(
+                    out=squares[:],
+                    in_=gen_sb[:, i * DIM : (i + 1) * DIM],
+                    func=FUNC.Square,
+                    accum_out=gen_sq[:, i : i + 1],
+                )
+
+        def transpose_gen(k):
+            gen_turned = psum_g.tile([P, PAIR * P], F32)
+            for a in range(PAIR):
+                i = k * PAIR + a
+                nc.tensor.transpose(
+                    gen_turned[:, a * P : (a + 1) * P], gen_words[:, i * WORDS : (i + 1) * WORDS], ident[:]
+                )
+            gen_t = gen_t_pool.tile([P, PAIR * P], F32)
+            nc.vector.tensor_copy(out=gen_t[:], in_=gen_turned[:])
+            gen_t_of[k] = gen_t
+
+        def distances(k):
+            halves = gen_t_of[k][:].bitcast(BF16).rearrange("w (a i h) -> w a i h", a=PAIR, h=HALVES)
+            dist = dist_pool.tile([P, PAIR, N_POS], F32)
+            for a in range(PAIR):
+                i = k * PAIR + a
+                v_ps = psum_v.tile([P, N_POS], F32)
+                for b in range(POS_TILES):
+                    nc.tensor.matmul(
+                        v_ps[:, b * P : (b + 1) * P],
+                        lhsT=neg_pos_sq[:, b * P : (b + 1) * P],
+                        rhs=ident[:],
+                        is_transpose=True,
+                        start=(b == 0),
+                        stop=False,
+                    )
+                for h in range(HALVES):
+                    nc.tensor.matmul(
+                        v_ps[:],
+                        lhsT=halves[:, a, :, h],
+                        rhs=pos2_t[:, h * N_POS : (h + 1) * N_POS],
+                        start=False,
+                        stop=(h == HALVES - 1),
+                    )
+                nc.vector.tensor_scalar(
+                    out=dist[:, a, :],
+                    in0=v_ps[:],
+                    scalar1=gen_sq[:, i : i + 1],
+                    scalar2=None,
+                    op0=ALU.min,
+                    op1=ALU.max,
+                    accum_out=v_max[:, i : i + 1],
+                )
+            dist_of[k] = dist
+            if k % BATCH == BATCH - 1:
+                cols = slice((k + 1 - BATCH) * PAIR, (k + 1) * PAIR)
+                nc.vector.tensor_tensor(
+                    out=s_min[:, cols], in0=gen_sq[:, cols], in1=v_max[:, cols], op=ALU.subtract
+                )
+
+        def roots(batch):
+            for k in range(batch * BATCH, (batch + 1) * BATCH):
+                for a in range(PAIR):
+                    i = k * PAIR + a
+                    nc.scalar.activation(
+                        out=dist_of[k][:, a, :],
+                        in_=dist_of[k][:, a, :],
+                        func=FUNC.Sqrt,
+                        scale=-1.0,
+                        bias=gen_sq[:, i : i + 1],
+                    )
+            lo = batch * BATCH * PAIR
+            hi = lo + BATCH * PAIR
+            nc.scalar.activation(out=d_min[:, lo:hi], in_=s_min[:, lo:hi], func=FUNC.Sqrt)
+            for t in range(N_T):
+                nc.scalar.mul(
+                    out=shift[:, t * TILES + lo : t * TILES + hi], in_=d_min[:, lo:hi], mul=1.0 / TEMPS[t]
+                )
+
+        def exps(k):
+            e_sb = e_pool.tile([P, N_T * PAIR * N_POS], BF16)
+            for t in range(N_T):
+                for a in range(PAIR):
+                    i = k * PAIR + a
+                    unit = t * PAIR + a
+                    nc.scalar.activation(
+                        out=e_sb[:, unit * N_POS : (unit + 1) * N_POS],
+                        in_=dist_of[k][:, a, :],
+                        func=FUNC.Exp,
+                        scale=-1.0 / TEMPS[t],
+                        bias=shift[:, t * TILES + i : t * TILES + i + 1],
+                        accum_out=row_sum[:, i * N_T + t : i * N_T + t + 1],
+                    )
+            e_of[k] = e_sb
+
+        def turn(k, t):
+            e_words = e_of[k][:].bitcast(F32)
+            turned = psum_turn.tile([P, PAIR * 2 * P], F32, tag="turned")
+            for q in range(PAIR * 2):
+                col = (t * PAIR * 2 + q) * P
+                nc.tensor.transpose(turned[:, q * P : (q + 1) * P], e_words[:, col : col + P], ident[:])
+            grouped = mx_pool.tile([P, PAIR * N_POS], BF16, align_bytes=64)
+            nc.vector.tensor_copy(
+                out=grouped[:].bitcast(F32).rearrange("w (a i u) -> w a i u", a=PAIR, u=2),
+                in_=turned[:].rearrange("w (a u i) -> w a i u", a=PAIR, u=2),
+            )
+            grouped_of[(k, t)] = grouped
+
+        def quantise(k, t):
+            codes = mx_pool.tile([P, PAIR * P], U32, align_bytes=64)
+            scales = mx_pool.tile([P, PAIR * P], U8, align_bytes=64)
+            nc.vector.quantize_mx(out=codes[:].bitcast(FP8X4), scales=scales[:], in_=grouped_of[(k, t)][:])
+            codes_of[(k, t)] = codes
+            scales_of[(k, t)] = scales
+
+        def denominators(k):
+            cols = slice(k * PAIR * N_T, (k + 1) * PAIR * N_T)
+            nc.vector.tensor_tensor(
+                out=denom[:, cols].rearrange("p (a t) -> p a t", a=PAIR),
+                in0=row_sum[:, cols].rearrange("p (a t) -> p a t", a=PAIR),
+                in1=drift[:].unsqueeze(1).to_broadcast([P, PAIR, N_T]),
+                op=ALU.mult,
+            )
+
+        def weights(k):
+            cols = slice(k * PAIR * N_T, (k + 1) * PAIR * N_T)
+            nc.vector.reciprocal(out=weight[:, cols], in_=denom[:, cols])
+
+        def products(k):
+            for t in range(N_T):
+                prod = psum_o.tile([P, PAIR * DIM], F32)
+                for a in range(PAIR):
+                    nc.tensor.matmul_mx(
+                        out=prod[:, a * DIM : (a + 1) * DIM],
+                        lhsT=codes_of[(k, t)][:, a * P : (a + 1) * P].bitcast(FP8X4),
+                        lhsT_scale=scales_of[(k, t)][:, a * P : (a + 1) * P],
+                        rhs=pos_codes[:].bitcast(FP8X4),
+                        rhs_scale=pos_scales[:],
+                        start=True,
+                        stop=True,
+                    )
+                prod_of[(k, t)] = prod
+
+        def combine(k):
+            res = res_pool.tile([P, PAIR * DIM], F32)
+            for t in range(N_T):
+                for a in range(PAIR):
+                    i = k * PAIR + a
+                    cols = slice(a * DIM, (a + 1) * DIM)
+                    w_col = weight[:, i * N_T + t : i * N_T + t + 1]
+                    if t == 0:
+                        nc.vector.tensor_scalar(
+                            out=res[:, cols], in0=prod_of[(k, t)][:, cols], scalar1=w_col, scalar2=None, op0=ALU.mult
+                        )
+                    else:
+                        nc.vector.scalar_tensor_tensor(
+                            out=res[:, cols],
+                            in0=prod_of[(k, t)][:, cols],
+                            scalar=w_col,
+                            in1=res[:, cols],
+                            op0=ALU.mult,
+                            op1=ALU.add,
+                        )
+            nc.sync.dma_start(out=out_rows[:, k * PAIR * DIM : (k + 1) * PAIR * DIM], in_=res[:])
+
+        def tick(s):
+            done = s - 1
+            far = s + AHEAD
+            if s < STEPS:
+                exps(s)
+            if far + 1 < STEPS:
+                norms(far + 1)
+            if done >= 0:
+                denominators(done)
+                turn(done, 0)
+                turn(done, 1)
+                weights(done)
+                quantise(done, 0)
+                turn(done, 2)
+                quantise(done, 1)
+            if far + 1 < STEPS:
+                transpose_gen(far + 1)
+            if done >= 0:
+                quantise(done, 2)
+            if far < STEPS:
+                distances(far)
+            if done >= 0:
+                products(done)
+                combine(done)
+
+        norms(0)
+        transpose_gen(0)
+        for k in range(AHEAD):
+            norms(k + 1)
+            transpose_gen(k + 1)
+            distances(k)
+
+        pos_grouped = const.tile([P, DIM * PACK], BF16, align_bytes=64)
+        nc.vector.tensor_copy(
+            out=pos_grouped[:].rearrange("w (c r) -> w c r", r=PACK),
+            in_=pos_k[:].rearrange("w (r c) -> w c r", r=PACK),
+        )
+        pos_codes = const.tile([P, DIM], U32, align_bytes=64)
+        pos_scales = const.tile([P, DIM], U8, align_bytes=64)
+        nc.vector.quantize_mx(out=pos_codes[:].bitcast(FP8X4), scales=pos_scales[:], in_=pos_grouped[:])
+
+        for batch in range(STEPS // BATCH):
+            roots(batch)
+            for s in range(batch * BATCH, (batch + 1) * BATCH):
+                tick(s)
+        tick(STEPS)

@@ -28,7 +28,7 @@ PACK = 4
 
 BATCH = 8
 AHEAD = BATCH + 3
-E_BUFS = 5
+E_BUFS = 4
 
 FLOPS = 2 * N_GEN * N_POS * DIM * (1 + N_T)
 
@@ -47,9 +47,8 @@ def tile_driftingfield_pa_t_kernel(tc, gen_features, pos_features, drift_scales,
         e_pool = ctx.enter_context(tc.tile_pool(name="e", bufs=E_BUFS))
         mx_pool = ctx.enter_context(tc.tile_pool(name="mx", bufs=N_T))
         res_pool = ctx.enter_context(tc.tile_pool(name="res", bufs=3))
-        psum_v = ctx.enter_context(tc.psum_pool(name="psum_v", bufs=2))
-        psum_g = ctx.enter_context(tc.psum_pool(name="psum_g", bufs=1))
-        psum_turn = ctx.enter_context(tc.psum_pool(name="psum_turn", bufs=2))
+        psum_v = ctx.enter_context(tc.psum_pool(name="psum_v", bufs=PAIR))
+        psum_turn = ctx.enter_context(tc.psum_pool(name="psum_turn", bufs=3))
         psum_o = ctx.enter_context(tc.psum_pool(name="psum_o", bufs=N_T))
 
         pos_rows = const.tile([P, POS_TILES * DIM], BF16)
@@ -123,9 +122,12 @@ def tile_driftingfield_pa_t_kernel(tc, gen_features, pos_features, drift_scales,
         drift = const.tile([P, N_T], F32)
         nc.vector.tensor_copy(out=drift[:], in_=scale_bf[:])
 
+        gen_turned_of = {}
         gen_t_of = {}
+        v_of = {}
         dist_of = {}
         e_of = {}
+        turned_of = {}
         grouped_of = {}
         codes_of = {}
         scales_of = {}
@@ -142,22 +144,23 @@ def tile_driftingfield_pa_t_kernel(tc, gen_features, pos_features, drift_scales,
                     accum_out=gen_sq[:, i : i + 1],
                 )
 
-        def transpose_gen(k):
-            gen_turned = psum_g.tile([P, PAIR * P], F32)
+        def turn_gen(k):
+            gen_turned = psum_turn.tile([P, PAIR * P], F32, tag="turned")
             for a in range(PAIR):
                 i = k * PAIR + a
                 nc.tensor.transpose(
                     gen_turned[:, a * P : (a + 1) * P], gen_words[:, i * WORDS : (i + 1) * WORDS], ident[:]
                 )
+            gen_turned_of[k] = gen_turned
+
+        def empty_gen(k):
             gen_t = gen_t_pool.tile([P, PAIR * P], F32)
-            nc.vector.tensor_copy(out=gen_t[:], in_=gen_turned[:])
+            nc.vector.tensor_copy(out=gen_t[:], in_=gen_turned_of[k][:])
             gen_t_of[k] = gen_t
 
-        def distances(k):
+        def gram(k):
             halves = gen_t_of[k][:].bitcast(BF16).rearrange("w (a i h) -> w a i h", a=PAIR, h=HALVES)
-            dist = dist_pool.tile([P, PAIR, N_POS], F32)
             for a in range(PAIR):
-                i = k * PAIR + a
                 v_ps = psum_v.tile([P, N_POS], F32)
                 for b in range(POS_TILES):
                     nc.tensor.matmul(
@@ -176,9 +179,15 @@ def tile_driftingfield_pa_t_kernel(tc, gen_features, pos_features, drift_scales,
                         start=False,
                         stop=(h == HALVES - 1),
                     )
+                v_of[(k, a)] = v_ps
+
+        def clamp(k):
+            dist = dist_pool.tile([P, PAIR, N_POS], F32)
+            for a in range(PAIR):
+                i = k * PAIR + a
                 nc.vector.tensor_scalar(
                     out=dist[:, a, :],
-                    in0=v_ps[:],
+                    in0=v_of[(k, a)][:],
                     scalar1=gen_sq[:, i : i + 1],
                     scalar2=None,
                     op0=ALU.min,
@@ -233,10 +242,13 @@ def tile_driftingfield_pa_t_kernel(tc, gen_features, pos_features, drift_scales,
             for q in range(PAIR * 2):
                 col = (t * PAIR * 2 + q) * P
                 nc.tensor.transpose(turned[:, q * P : (q + 1) * P], e_words[:, col : col + P], ident[:])
+            turned_of[(k, t)] = turned
+
+        def empty(k, t):
             grouped = mx_pool.tile([P, PAIR * N_POS], BF16, align_bytes=64)
             nc.vector.tensor_copy(
                 out=grouped[:].bitcast(F32).rearrange("w (a i u) -> w a i u", a=PAIR, u=2),
-                in_=turned[:].rearrange("w (a u i) -> w a i u", a=PAIR, u=2),
+                in_=turned_of[(k, t)][:].rearrange("w (a u i) -> w a i u", a=PAIR, u=2),
             )
             grouped_of[(k, t)] = grouped
 
@@ -297,37 +309,46 @@ def tile_driftingfield_pa_t_kernel(tc, gen_features, pos_features, drift_scales,
                         )
             nc.sync.dma_start(out=out_rows[:, k * PAIR * DIM : (k + 1) * PAIR * DIM], in_=res[:])
 
-        def tick(s):
-            done = s - 1
-            far = s + AHEAD
-            if s < STEPS:
-                exps(s)
+        def tick(k):
+            far = k + 1 + AHEAD
+            live = 0 <= k < STEPS
             if far + 1 < STEPS:
                 norms(far + 1)
-            if done >= 0:
-                denominators(done)
-                turn(done, 0)
-                turn(done, 1)
-                weights(done)
-                quantise(done, 0)
-                turn(done, 2)
-                quantise(done, 1)
-            if far + 1 < STEPS:
-                transpose_gen(far + 1)
-            if done >= 0:
-                quantise(done, 2)
+            if live:
+                denominators(k)
+                empty(k, 0)
+                empty(k, 1)
+                weights(k)
+                quantise(k, 0)
+                empty(k, 2)
+                quantise(k, 1)
             if far < STEPS:
-                distances(far)
-            if done >= 0:
-                products(done)
-                combine(done)
+                gram(far)
+            if far + 1 < STEPS:
+                turn_gen(far + 1)
+            if k >= 1:
+                combine(k - 1)
+            if live:
+                quantise(k, 2)
+            if far + 1 < STEPS:
+                empty_gen(far + 1)
+            if far < STEPS:
+                clamp(far)
+            if k + 1 < STEPS:
+                for t in range(N_T):
+                    turn(k + 1, t)
+            if live:
+                products(k)
 
         norms(0)
-        transpose_gen(0)
+        turn_gen(0)
+        empty_gen(0)
         for k in range(AHEAD):
             norms(k + 1)
-            transpose_gen(k + 1)
-            distances(k)
+            turn_gen(k + 1)
+            empty_gen(k + 1)
+            gram(k)
+            clamp(k)
 
         pos_grouped = const.tile([P, DIM * PACK], BF16, align_bytes=64)
         nc.vector.tensor_copy(
@@ -341,5 +362,7 @@ def tile_driftingfield_pa_t_kernel(tc, gen_features, pos_features, drift_scales,
         for batch in range(STEPS // BATCH):
             roots(batch)
             for s in range(batch * BATCH, (batch + 1) * BATCH):
-                tick(s)
+                exps(s)
+                tick(s - 1)
+        tick(STEPS - 1)
         tick(STEPS)

@@ -294,7 +294,11 @@ def tile_driftingfield_pa_t_kernel(tc, gen_features, pos_features, drift_scales,
                     i = k * PAIR + a
                     cols = slice(a * DIM, (a + 1) * DIM)
                     w_col = weight[:, i * N_T + t : i * N_T + t + 1]
-                    if t == 0:
+                    if t == 0 and k >= STEPS - BATCH:
+                        nc.scalar.activation(
+                            out=res[:, cols], in_=prod_of[(k, t)][:, cols], func=FUNC.Copy, scale=w_col
+                        )
+                    elif t == 0:
                         nc.vector.tensor_scalar(
                             out=res[:, cols], in0=prod_of[(k, t)][:, cols], scalar1=w_col, scalar2=None, op0=ALU.mult
                         )

@@ -145,8 +145,8 @@ def tile_driftingfield_pa_t_kernel(tc, gen_features, pos_features, drift_scales,
                 )
 
         def turn_gen(k):
-            gen_turned = psum_turn.tile([P, PAIR * P], F32, tag="turned")
-            for a in range(PAIR):
+            gen_turned = psum_turn.tile([P, 2 * PAIR * P], F32, tag="turned")
+            for a in range(2 * PAIR):
                 i = k * PAIR + a
                 nc.tensor.transpose(
                     gen_turned[:, a * P : (a + 1) * P], gen_words[:, i * WORDS : (i + 1) * WORDS], ident[:]
@@ -154,12 +154,12 @@ def tile_driftingfield_pa_t_kernel(tc, gen_features, pos_features, drift_scales,
             gen_turned_of[k] = gen_turned
 
         def empty_gen(k):
-            gen_t = gen_t_pool.tile([P, PAIR * P], F32)
+            gen_t = gen_t_pool.tile([P, 2 * PAIR * P], F32)
             nc.vector.tensor_copy(out=gen_t[:], in_=gen_turned_of[k][:])
             gen_t_of[k] = gen_t
 
         def gram(k):
-            halves = gen_t_of[k][:].bitcast(BF16).rearrange("w (a i h) -> w a i h", a=PAIR, h=HALVES)
+            halves = gen_t_of[k - k % 2][:].bitcast(BF16).rearrange("w (a i h) -> w a i h", a=2 * PAIR, h=HALVES)
             for a in range(PAIR):
                 v_ps = psum_v.tile([P, N_POS], F32)
                 for b in range(POS_TILES):
@@ -174,7 +174,7 @@ def tile_driftingfield_pa_t_kernel(tc, gen_features, pos_features, drift_scales,
                 for h in range(HALVES):
                     nc.tensor.matmul(
                         v_ps[:],
-                        lhsT=halves[:, a, :, h],
+                        lhsT=halves[:, k % 2 * PAIR + a, :, h],
                         rhs=pos2_t[:, h * N_POS : (h + 1) * N_POS],
                         start=False,
                         stop=(h == HALVES - 1),
@@ -260,16 +260,16 @@ def tile_driftingfield_pa_t_kernel(tc, gen_features, pos_features, drift_scales,
             scales_of[(k, t)] = scales
 
         def denominators(k):
-            cols = slice(k * PAIR * N_T, (k + 1) * PAIR * N_T)
+            cols = slice(k * PAIR * N_T, (k + 2) * PAIR * N_T)
             nc.vector.tensor_tensor(
-                out=denom[:, cols].rearrange("p (a t) -> p a t", a=PAIR),
-                in0=row_sum[:, cols].rearrange("p (a t) -> p a t", a=PAIR),
-                in1=drift[:].unsqueeze(1).to_broadcast([P, PAIR, N_T]),
+                out=denom[:, cols].rearrange("p (a t) -> p a t", t=N_T),
+                in0=row_sum[:, cols].rearrange("p (a t) -> p a t", t=N_T),
+                in1=drift[:].unsqueeze(1).to_broadcast([P, 2 * PAIR, N_T]),
                 op=ALU.mult,
             )
 
         def weights(k):
-            cols = slice(k * PAIR * N_T, (k + 1) * PAIR * N_T)
+            cols = slice(k * PAIR * N_T, (k + 2) * PAIR * N_T)
             nc.vector.reciprocal(out=weight[:, cols], in_=denom[:, cols])
 
         def products(k):
@@ -319,25 +319,26 @@ def tile_driftingfield_pa_t_kernel(tc, gen_features, pos_features, drift_scales,
             if far + 1 < STEPS:
                 norms(far + 1)
             if live:
-                denominators(k)
                 empty(k, 0)
                 empty(k, 1)
-                weights(k)
                 quantise(k, 0)
                 empty(k, 2)
                 quantise(k, 1)
+            if far + 2 < STEPS and far % 2 == 0:
+                turn_gen(far + 2)
+                empty_gen(far + 2)
             if far < STEPS:
                 gram(far)
-            if far + 1 < STEPS:
-                turn_gen(far + 1)
+            if live and k % 2 == 0:
+                denominators(k)
             if k >= 1:
                 combine(k - 1)
             if live:
                 quantise(k, 2)
-            if far + 1 < STEPS:
-                empty_gen(far + 1)
             if far < STEPS:
                 clamp(far)
+            if live and k % 2 == 0:
+                weights(k)
             if k + 1 < STEPS:
                 for t in range(N_T):
                     turn(k + 1, t)
@@ -349,8 +350,9 @@ def tile_driftingfield_pa_t_kernel(tc, gen_features, pos_features, drift_scales,
         empty_gen(0)
         for k in range(AHEAD):
             norms(k + 1)
-            turn_gen(k + 1)
-            empty_gen(k + 1)
+            if k % 2 == 0:
+                turn_gen(k + 2)
+                empty_gen(k + 2)
             gram(k)
             clamp(k)
 

@@ -28,6 +28,8 @@ PACK = 4
 
 BATCH = 8
 AHEAD = BATCH + 3
+FREE = (20, 25)
+PARTS = 32
 E_BUFS = 4
 
 FLOPS = 2 * N_GEN * N_POS * DIM * (1 + N_T)
@@ -43,6 +45,7 @@ def tile_driftingfield_pa_t_kernel(tc, gen_features, pos_features, drift_scales,
         const = ctx.enter_context(tc.tile_pool(name="const", bufs=1))
         junk_pool = ctx.enter_context(tc.tile_pool(name="junk", bufs=4))
         gen_t_pool = ctx.enter_context(tc.tile_pool(name="gen_t", bufs=3))
+        part_pool = ctx.enter_context(tc.tile_pool(name="part", bufs=2))
         dist_pool = ctx.enter_context(tc.tile_pool(name="dist", bufs=AHEAD + 1))
         e_pool = ctx.enter_context(tc.tile_pool(name="e", bufs=E_BUFS))
         mx_pool = ctx.enter_context(tc.tile_pool(name="mx", bufs=N_T))
@@ -78,6 +81,7 @@ def tile_driftingfield_pa_t_kernel(tc, gen_features, pos_features, drift_scales,
         nc.scalar.activation(out=warm[:], in_=warm[:], func=FUNC.Sqrt)
 
         gen_sq = const.tile([P, TILES], F32)
+        parts = const.tile([P, (FREE[1] - FREE[0]) * PAIR, PARTS], F32)
         v_max = const.tile([P, TILES], F32)
         s_min = const.tile([P, TILES], F32)
         d_min = const.tile([P, TILES], F32)
@@ -95,15 +99,6 @@ def tile_driftingfield_pa_t_kernel(tc, gen_features, pos_features, drift_scales,
                 func=FUNC.Square,
                 accum_out=pos_sq[:, b : b + 1],
             )
-        neg_pos_sq = const.tile([P, POS_TILES * P], F32)
-        nc.vector.tensor_scalar(
-            out=neg_pos_sq[:].rearrange("p (b c) -> p b c", b=POS_TILES),
-            in0=pos_sq[:].unsqueeze(2).to_broadcast([P, POS_TILES, P]),
-            scalar1=-1.0,
-            scalar2=None,
-            op0=ALU.mult,
-        )
-
         pos_words = pos_rows[:].bitcast(F32)
         pos_turned = psum_turn.tile([P, POS_TILES * P], F32, tag="turned")
         for b in range(POS_TILES):
@@ -115,6 +110,15 @@ def tile_driftingfield_pa_t_kernel(tc, gen_features, pos_features, drift_scales,
             out=pos2_t[:].rearrange("w (h j) -> w h j", h=HALVES),
             in0=pos_turned[:].bitcast(BF16).rearrange("w (j h) -> w h j", h=HALVES),
             scalar1=2.0,
+            scalar2=None,
+            op0=ALU.mult,
+        )
+
+        neg_pos_sq = const.tile([P, POS_TILES * P], F32)
+        nc.vector.tensor_scalar(
+            out=neg_pos_sq[:].rearrange("p (b c) -> p b c", b=POS_TILES),
+            in0=pos_sq[:].unsqueeze(2).to_broadcast([P, POS_TILES, P]),
+            scalar1=-1.0,
             scalar2=None,
             op0=ALU.mult,
         )
@@ -143,6 +147,24 @@ def tile_driftingfield_pa_t_kernel(tc, gen_features, pos_features, drift_scales,
                     func=FUNC.Square,
                     accum_out=gen_sq[:, i : i + 1],
                 )
+
+        def norms_gpsimd(k):
+            squares = part_pool.tile([P, PAIR, DIM], F32)
+            rows = gen_sb[:, k * PAIR * DIM : (k + 1) * PAIR * DIM].rearrange("p (a d) -> p a d", a=PAIR)
+            nc.gpsimd.tensor_tensor(out=squares[:], in0=rows, in1=rows, op=ALU.mult)
+            lo = (k - FREE[0]) * PAIR
+            half = DIM // 2
+            while half >= PARTS:
+                sums = squares[:, :, 0:half] if half > PARTS else parts[:, lo : lo + PAIR, :]
+                nc.gpsimd.tensor_tensor(
+                    out=sums, in0=squares[:, :, 0:half], in1=squares[:, :, half : 2 * half], op=ALU.add
+                )
+                half //= 2
+
+        def sum_parts():
+            nc.vector.tensor_reduce(
+                out=gen_sq[:, FREE[0] * PAIR : FREE[1] * PAIR], in_=parts[:], axis=mybir.AxisListType.X, op=ALU.add
+            )
 
         def turn_gen(k):
             gen_turned = psum_turn.tile([P, 2 * PAIR * P], F32, tag="turned")
@@ -212,6 +234,8 @@ def tile_driftingfield_pa_t_kernel(tc, gen_features, pos_features, drift_scales,
                         scale=-1.0,
                         bias=gen_sq[:, i : i + 1],
                     )
+                if batch == 0:
+                    norms(AHEAD + 1 + k)
             lo = batch * BATCH * PAIR
             hi = lo + BATCH * PAIR
             nc.scalar.activation(out=d_min[:, lo:hi], in_=s_min[:, lo:hi], func=FUNC.Sqrt)
@@ -316,8 +340,10 @@ def tile_driftingfield_pa_t_kernel(tc, gen_features, pos_features, drift_scales,
         def tick(k):
             far = k + 1 + AHEAD
             live = 0 <= k < STEPS
-            if far + 1 < STEPS:
-                norms(far + 1)
+            if 0 <= k < STEPS - FREE[1]:
+                norms(FREE[1] + k)
+            if k == 2:
+                sum_parts()
             if live:
                 empty(k, 0)
                 empty(k, 1)
@@ -345,6 +371,8 @@ def tile_driftingfield_pa_t_kernel(tc, gen_features, pos_features, drift_scales,
             if live:
                 products(k)
 
+        for k in range(FREE[0], FREE[1]):
+            norms_gpsimd(k)
         norms(0)
         turn_gen(0)
         empty_gen(0)

@@ -26,11 +26,24 @@ WORDS = DIM // 2
 HALVES = 2
 PACK = 4
 
-BATCH = 8
-AHEAD = BATCH + 3
+ENDS = (4, 10, 17, 24, 32)
+BATCHES = tuple(zip((0,) + ENDS[:-1], ENDS))
+HEAD = 8
+PACE = 2
+NLEAD = 2
+DIST_BUFS = 16
+AHEAD = 10
 FREE = (20, 25)
 PARTS = 32
-E_BUFS = 4
+LAST_TERM = 24
+WARM1 = 4
+WARM2 = 3
+SPLIT = 2
+FIRST_LOAD = 4
+TAIL_E = 30
+TAIL_E2 = 30
+LEAD = 1
+E_BUFS = 6
 
 FLOPS = 2 * N_GEN * N_POS * DIM * (1 + N_T)
 
@@ -46,7 +59,7 @@ def tile_driftingfield_pa_t_kernel(tc, gen_features, pos_features, drift_scales,
         junk_pool = ctx.enter_context(tc.tile_pool(name="junk", bufs=4))
         gen_t_pool = ctx.enter_context(tc.tile_pool(name="gen_t", bufs=3))
         part_pool = ctx.enter_context(tc.tile_pool(name="part", bufs=2))
-        dist_pool = ctx.enter_context(tc.tile_pool(name="dist", bufs=AHEAD + 1))
+        dist_pool = ctx.enter_context(tc.tile_pool(name="dist", bufs=DIST_BUFS))
         e_pool = ctx.enter_context(tc.tile_pool(name="e", bufs=E_BUFS))
         mx_pool = ctx.enter_context(tc.tile_pool(name="mx", bufs=N_T))
         res_pool = ctx.enter_context(tc.tile_pool(name="res", bufs=3))
@@ -61,7 +74,10 @@ def tile_driftingfield_pa_t_kernel(tc, gen_features, pos_features, drift_scales,
         )
         gen_sb = const.tile([P, TILES * DIM], BF16)
         load_cols = 8 * DIM
-        nc.sync.dma_start(out=gen_sb[:, 0:load_cols], in_=gen_rows[:, 0:load_cols])
+        first_cols = FIRST_LOAD * DIM
+        nc.sync.dma_start(out=gen_sb[:, 0:first_cols], in_=gen_rows[:, 0:first_cols])
+        if first_cols < load_cols:
+            nc.sync.dma_start(out=gen_sb[:, first_cols:load_cols], in_=gen_rows[:, first_cols:load_cols])
         pos_k = const.tile([P, PACK * DIM], BF16)
         nc.sync.dma_start(
             out=pos_k[:].rearrange("w (u r) -> w u r", u=2),
@@ -100,20 +116,29 @@ def tile_driftingfield_pa_t_kernel(tc, gen_features, pos_features, drift_scales,
                 accum_out=pos_sq[:, b : b + 1],
             )
         pos_words = pos_rows[:].bitcast(F32)
+        idle = const.tile([P, N_POS], BF16)
+        nc.vector.memset(idle[:], 0.0)
+        idle_ps = psum_o.tile([P, N_POS], F32, tag="prod")
+
+        def keep_warm(count):
+            for n in range(count):
+                nc.tensor.matmul(idle_ps[:], lhsT=idle[:, 0:P], rhs=idle[:], start=True, stop=True)
+
+        keep_warm(WARM1)
         pos_turned = psum_turn.tile([P, POS_TILES * P], F32, tag="turned")
         for b in range(POS_TILES):
             nc.tensor.transpose(
                 pos_turned[:, b * P : (b + 1) * P], pos_words[:, b * WORDS : (b + 1) * WORDS], ident[:]
             )
         pos2_t = const.tile([P, HALVES * N_POS], BF16)
-        nc.vector.tensor_scalar(
-            out=pos2_t[:].rearrange("w (h j) -> w h j", h=HALVES),
-            in0=pos_turned[:].bitcast(BF16).rearrange("w (j h) -> w h j", h=HALVES),
-            scalar1=2.0,
-            scalar2=None,
-            op0=ALU.mult,
-        )
-
+        keep_warm(WARM2)
+        pos_halves = pos_turned[:].bitcast(BF16).rearrange("w (j h) -> w h j", h=HALVES)
+        for h in range(HALVES):
+            pos2_h = pos2_t[:, h * N_POS : (h + 1) * N_POS]
+            if h < SPLIT:
+                nc.vector.tensor_scalar(out=pos2_h, in0=pos_halves[:, h, :], scalar1=2.0, scalar2=None, op0=ALU.mult)
+            else:
+                nc.scalar.activation(out=pos2_h, in_=pos_halves[:, h, :], func=FUNC.Copy, scale=2.0)
         neg_pos_sq = const.tile([P, POS_TILES * P], F32)
         nc.vector.tensor_scalar(
             out=neg_pos_sq[:].rearrange("p (b c) -> p b c", b=POS_TILES),
@@ -217,14 +242,15 @@ def tile_driftingfield_pa_t_kernel(tc, gen_features, pos_features, drift_scales,
                     accum_out=v_max[:, i : i + 1],
                 )
             dist_of[k] = dist
-            if k % BATCH == BATCH - 1:
-                cols = slice((k + 1 - BATCH) * PAIR, (k + 1) * PAIR)
-                nc.vector.tensor_tensor(
-                    out=s_min[:, cols], in0=gen_sq[:, cols], in1=v_max[:, cols], op=ALU.subtract
-                )
+            for first, end in BATCHES:
+                if k == end - 1:
+                    cols = slice(first * PAIR, end * PAIR)
+                    nc.vector.tensor_tensor(
+                        out=s_min[:, cols], in0=gen_sq[:, cols], in1=v_max[:, cols], op=ALU.subtract
+                    )
 
-        def roots(batch):
-            for k in range(batch * BATCH, (batch + 1) * BATCH):
+        def roots(first, end):
+            for k in range(first, end):
                 for a in range(PAIR):
                     i = k * PAIR + a
                     nc.scalar.activation(
@@ -234,10 +260,7 @@ def tile_driftingfield_pa_t_kernel(tc, gen_features, pos_features, drift_scales,
                         scale=-1.0,
                         bias=gen_sq[:, i : i + 1],
                     )
-                if batch == 0:
-                    norms(AHEAD + 1 + k)
-            lo = batch * BATCH * PAIR
-            hi = lo + BATCH * PAIR
+            lo, hi = first * PAIR, end * PAIR
             nc.scalar.activation(out=d_min[:, lo:hi], in_=s_min[:, lo:hi], func=FUNC.Sqrt)
             for t in range(N_T):
                 nc.scalar.mul(
@@ -269,19 +292,40 @@ def tile_driftingfield_pa_t_kernel(tc, gen_features, pos_features, drift_scales,
             turned_of[(k, t)] = turned
 
         def empty(k, t):
-            grouped = mx_pool.tile([P, PAIR * N_POS], BF16, align_bytes=64)
-            nc.vector.tensor_copy(
-                out=grouped[:].bitcast(F32).rearrange("w (a i u) -> w a i u", a=PAIR, u=2),
+            if t == 1:
+                grouped = grouped_of[(k, 0)]
+            elif t == 0:
+                grouped = mx_pool.tile([P, 2 * PAIR * N_POS], BF16, align_bytes=64, tag="grouped_two", bufs=2)
+            else:
+                grouped = mx_pool.tile([P, PAIR * N_POS], BF16, align_bytes=64, tag="grouped_one", bufs=2)
+            part = grouped[:, (t % 2) * PAIR * N_POS : (t % 2 + 1) * PAIR * N_POS] if t < 2 else grouped[:]
+            on_scalar = (t == 0 and k >= TAIL_E) or (t == 1 and k >= TAIL_E2)
+            copy = nc.scalar.copy if on_scalar else nc.vector.tensor_copy
+            copy(
+                out=part.bitcast(F32).rearrange("w (a i u) -> w a i u", a=PAIR, u=2),
                 in_=turned_of[(k, t)][:].rearrange("w (a u i) -> w a i u", a=PAIR, u=2),
             )
             grouped_of[(k, t)] = grouped
 
         def quantise(k, t):
-            codes = mx_pool.tile([P, PAIR * P], U32, align_bytes=64)
-            scales = mx_pool.tile([P, PAIR * P], U8, align_bytes=64)
+            width = PAIR * P * (2 if t == 0 else 1)
+            codes = mx_pool.tile([P, width], U32, align_bytes=64, tag="codes_%d" % t, bufs=2)
+            scales = mx_pool.tile([P, width], U8, align_bytes=64, tag="scales_%d" % t, bufs=2)
             nc.vector.quantize_mx(out=codes[:].bitcast(FP8X4), scales=scales[:], in_=grouped_of[(k, t)][:])
-            codes_of[(k, t)] = codes
-            scales_of[(k, t)] = scales
+            for n in range(width // (PAIR * P)):
+                codes_of[(k, t + n)] = codes[:, n * PAIR * P : (n + 1) * PAIR * P]
+                scales_of[(k, t + n)] = scales[:, n * PAIR * P : (n + 1) * PAIR * P]
+
+        pos_codes = const.tile([P, DIM], U32, align_bytes=64)
+        pos_scales = const.tile([P, DIM], U8, align_bytes=64)
+
+        def quantise_pos():
+            pos_grouped = const.tile([P, DIM * PACK], BF16, align_bytes=64)
+            nc.vector.tensor_copy(
+                out=pos_grouped[:].rearrange("w (c r) -> w c r", r=PACK),
+                in_=pos_k[:].rearrange("w (r c) -> w c r", r=PACK),
+            )
+            nc.vector.quantize_mx(out=pos_codes[:].bitcast(FP8X4), scales=pos_scales[:], in_=pos_grouped[:])
 
         def denominators(k):
             cols = slice(k * PAIR * N_T, (k + 2) * PAIR * N_T)
@@ -298,7 +342,7 @@ def tile_driftingfield_pa_t_kernel(tc, gen_features, pos_features, drift_scales,
 
         def products(k):
             for t in range(N_T):
-                prod = psum_o.tile([P, PAIR * DIM], F32)
+                prod = psum_o.tile([P, PAIR * DIM], F32, tag="prod")
                 for a in range(PAIR):
                     nc.tensor.matmul_mx(
                         out=prod[:, a * DIM : (a + 1) * DIM],
@@ -318,7 +362,7 @@ def tile_driftingfield_pa_t_kernel(tc, gen_features, pos_features, drift_scales,
                     i = k * PAIR + a
                     cols = slice(a * DIM, (a + 1) * DIM)
                     w_col = weight[:, i * N_T + t : i * N_T + t + 1]
-                    if t == 0 and k >= STEPS - BATCH:
+                    if t == 0 and k >= LAST_TERM:
                         nc.scalar.activation(
                             out=res[:, cols], in_=prod_of[(k, t)][:, cols], func=FUNC.Copy, scale=w_col
                         )
@@ -337,35 +381,41 @@ def tile_driftingfield_pa_t_kernel(tc, gen_features, pos_features, drift_scales,
                         )
             nc.sync.dma_start(out=out_rows[:, k * PAIR * DIM : (k + 1) * PAIR * DIM], in_=res[:])
 
+        def made(k):
+            return min(HEAD + PACE * max(k + 1 + LEAD, 0), AHEAD + k + 1, STEPS) if k >= -1 - LEAD else HEAD
+
         def tick(k):
-            far = k + 1 + AHEAD
+            new = range(made(k), made(k + 1))
             live = 0 <= k < STEPS
-            if 0 <= k < STEPS - FREE[1]:
-                norms(FREE[1] + k)
+            for j in range(made(k + NLEAD), made(k + NLEAD + 1)):
+                if not FREE[0] <= j < FREE[1]:
+                    norms(j)
             if k == 2:
                 sum_parts()
             if live:
                 empty(k, 0)
                 empty(k, 1)
-                quantise(k, 0)
                 empty(k, 2)
-                quantise(k, 1)
-            if far + 2 < STEPS and far % 2 == 0:
-                turn_gen(far + 2)
-                empty_gen(far + 2)
-            if far < STEPS:
-                gram(far)
+                quantise(k, 0)
+            for far in new:
+                if far % 2 == 0 and far + 2 < STEPS:
+                    turn_gen(far + 2)
+                    empty_gen(far + 2)
+                if far == made(k):
+                    gram(far)
             if live and k % 2 == 0:
                 denominators(k)
             if k >= 1:
                 combine(k - 1)
             if live:
                 quantise(k, 2)
-            if far < STEPS:
+            for far in new:
+                if far > made(k):
+                    gram(far)
                 clamp(far)
             if live and k % 2 == 0:
                 weights(k)
-            if k + 1 < STEPS:
+            if 0 <= k + 1 < STEPS:
                 for t in range(N_T):
                     turn(k + 1, t)
             if live:
@@ -373,30 +423,23 @@ def tile_driftingfield_pa_t_kernel(tc, gen_features, pos_features, drift_scales,
 
         for k in range(FREE[0], FREE[1]):
             norms_gpsimd(k)
-        norms(0)
+        for k in range(made(-1 - LEAD + NLEAD)):
+            norms(k)
         turn_gen(0)
         empty_gen(0)
-        for k in range(AHEAD):
-            norms(k + 1)
+        for k in range(HEAD):
             if k % 2 == 0:
                 turn_gen(k + 2)
                 empty_gen(k + 2)
             gram(k)
             clamp(k)
+            if k == 1:
+                quantise_pos()
 
-        pos_grouped = const.tile([P, DIM * PACK], BF16, align_bytes=64)
-        nc.vector.tensor_copy(
-            out=pos_grouped[:].rearrange("w (c r) -> w c r", r=PACK),
-            in_=pos_k[:].rearrange("w (r c) -> w c r", r=PACK),
-        )
-        pos_codes = const.tile([P, DIM], U32, align_bytes=64)
-        pos_scales = const.tile([P, DIM], U8, align_bytes=64)
-        nc.vector.quantize_mx(out=pos_codes[:].bitcast(FP8X4), scales=pos_scales[:], in_=pos_grouped[:])
-
-        for batch in range(STEPS // BATCH):
-            roots(batch)
-            for s in range(batch * BATCH, (batch + 1) * BATCH):
+        for first, end in BATCHES:
+            roots(first, end)
+            for s in range(first, end):
                 exps(s)
-                tick(s - 1)
-        tick(STEPS - 1)
-        tick(STEPS)
+                tick(s - 1 - LEAD)
+        for k in range(STEPS - 1 - LEAD, STEPS + 1):
+            tick(k)

@@ -26,17 +26,18 @@ WORDS = DIM // 2
 HALVES = 2
 PACK = 4
 
-ENDS = (4, 10, 17, 24, 32)
+ENDS = (6, 14, 23, 32)
 BATCHES = tuple(zip((0,) + ENDS[:-1], ENDS))
 HEAD = 8
 PACE = 2
 NLEAD = 2
-DIST_BUFS = 16
-AHEAD = 10
-FREE = (20, 25)
+DIST_BUFS = 18
+AHEAD = 11
+FREE = (14, 20)
 PARTS = 32
-LAST_TERM = 24
-WARM1 = 4
+LAST_TERM = 25
+SUM_AT = 1
+WARM1 = 3
 WARM2 = 3
 SPLIT = 2
 FIRST_LOAD = 4
@@ -390,7 +391,7 @@ def tile_driftingfield_pa_t_kernel(tc, gen_features, pos_features, drift_scales,
             for j in range(made(k + NLEAD), made(k + NLEAD + 1)):
                 if not FREE[0] <= j < FREE[1]:
                     norms(j)
-            if k == 2:
+            if k == SUM_AT:
                 sum_parts()
             if live:
                 empty(k, 0)

@@ -33,10 +33,7 @@ PACE = 2
 NLEAD = 2
 DIST_BUFS = 18
 AHEAD = 11
-FREE = (14, 20)
-PARTS = 32
 LAST_TERM = 25
-SUM_AT = 1
 WARM1 = 3
 WARM2 = 3
 SPLIT = 2
@@ -59,7 +56,6 @@ def tile_driftingfield_pa_t_kernel(tc, gen_features, pos_features, drift_scales,
         const = ctx.enter_context(tc.tile_pool(name="const", bufs=1))
         junk_pool = ctx.enter_context(tc.tile_pool(name="junk", bufs=4))
         gen_t_pool = ctx.enter_context(tc.tile_pool(name="gen_t", bufs=3))
-        part_pool = ctx.enter_context(tc.tile_pool(name="part", bufs=2))
         dist_pool = ctx.enter_context(tc.tile_pool(name="dist", bufs=DIST_BUFS))
         e_pool = ctx.enter_context(tc.tile_pool(name="e", bufs=E_BUFS))
         mx_pool = ctx.enter_context(tc.tile_pool(name="mx", bufs=N_T))
@@ -98,7 +94,6 @@ def tile_driftingfield_pa_t_kernel(tc, gen_features, pos_features, drift_scales,
         nc.scalar.activation(out=warm[:], in_=warm[:], func=FUNC.Sqrt)
 
         gen_sq = const.tile([P, TILES], F32)
-        parts = const.tile([P, (FREE[1] - FREE[0]) * PAIR, PARTS], F32)
         v_max = const.tile([P, TILES], F32)
         s_min = const.tile([P, TILES], F32)
         d_min = const.tile([P, TILES], F32)
@@ -173,24 +168,6 @@ def tile_driftingfield_pa_t_kernel(tc, gen_features, pos_features, drift_scales,
                     func=FUNC.Square,
                     accum_out=gen_sq[:, i : i + 1],
                 )
-
-        def norms_gpsimd(k):
-            squares = part_pool.tile([P, PAIR, DIM], F32)
-            rows = gen_sb[:, k * PAIR * DIM : (k + 1) * PAIR * DIM].rearrange("p (a d) -> p a d", a=PAIR)
-            nc.gpsimd.tensor_tensor(out=squares[:], in0=rows, in1=rows, op=ALU.mult)
-            lo = (k - FREE[0]) * PAIR
-            half = DIM // 2
-            while half >= PARTS:
-                sums = squares[:, :, 0:half] if half > PARTS else parts[:, lo : lo + PAIR, :]
-                nc.gpsimd.tensor_tensor(
-                    out=sums, in0=squares[:, :, 0:half], in1=squares[:, :, half : 2 * half], op=ALU.add
-                )
-                half //= 2
-
-        def sum_parts():
-            nc.vector.tensor_reduce(
-                out=gen_sq[:, FREE[0] * PAIR : FREE[1] * PAIR], in_=parts[:], axis=mybir.AxisListType.X, op=ALU.add
-            )
 
         def turn_gen(k):
             gen_turned = psum_turn.tile([P, 2 * PAIR * P], F32, tag="turned")
@@ -389,10 +366,7 @@ def tile_driftingfield_pa_t_kernel(tc, gen_features, pos_features, drift_scales,
             new = range(made(k), made(k + 1))
             live = 0 <= k < STEPS
             for j in range(made(k + NLEAD), made(k + NLEAD + 1)):
-                if not FREE[0] <= j < FREE[1]:
-                    norms(j)
-            if k == SUM_AT:
-                sum_parts()
+                norms(j)
             if live:
                 empty(k, 0)
                 empty(k, 1)
@@ -422,8 +396,6 @@ def tile_driftingfield_pa_t_kernel(tc, gen_features, pos_features, drift_scales,
             if live:
                 products(k)
 
-        for k in range(FREE[0], FREE[1]):
-            norms_gpsimd(k)
         for k in range(made(-1 - LEAD + NLEAD)):
             norms(k)
         turn_gen(0)

from contextlib import ExitStack

import concourse.mybir as mybir
from concourse.masks import make_identity

F32 = mybir.dt.float32
BF16 = mybir.dt.bfloat16
U32 = mybir.dt.uint32
U8 = mybir.dt.uint8
FP8X4 = mybir.dt.float8_e4m3fn_x4
FUNC = mybir.ActivationFunctionType
ALU = mybir.AluOpType

P = 128
N_GEN = 8192
N_POS = 512
DIM = 256
TEMPS = (0.02, 0.05, 0.2)
N_T = len(TEMPS)

TILES = N_GEN // P
PAIR = 2
STEPS = TILES // PAIR
POS_TILES = N_POS // P
WORDS = DIM // 2
HALVES = 2
PACK = 4

ENDS = (6, 14, 23, 32)
BATCHES = tuple(zip((0,) + ENDS[:-1], ENDS))
HEAD = 8
PACE = 2
NLEAD = 2
DIST_BUFS = 18
AHEAD = 11
LAST_TERM = 25
WARM1 = 3
WARM2 = 3
SPLIT = 2
FIRST_LOAD = 4
TAIL_E = 30
TAIL_E2 = 30
LEAD = 1
E_BUFS = 6

FLOPS = 2 * N_GEN * N_POS * DIM * (1 + N_T)


def tile_driftingfield_pa_t_kernel(tc, gen_features, pos_features, drift_scales, out):
    nc = tc.nc
    gen_rows = gen_features.rearrange("(p t) d -> p (t d)", t=TILES)
    out_rows = out.rearrange("(p t) d -> p (t d)", t=TILES)

    with ExitStack() as ctx:
        ctx.enter_context(tc.manual_schedule())
        const = ctx.enter_context(tc.tile_pool(name="const", bufs=1))
        junk_pool = ctx.enter_context(tc.tile_pool(name="junk", bufs=4))
        gen_t_pool = ctx.enter_context(tc.tile_pool(name="gen_t", bufs=3))
        dist_pool = ctx.enter_context(tc.tile_pool(name="dist", bufs=DIST_BUFS))
        e_pool = ctx.enter_context(tc.tile_pool(name="e", bufs=E_BUFS))
        mx_pool = ctx.enter_context(tc.tile_pool(name="mx", bufs=N_T))
        res_pool = ctx.enter_context(tc.tile_pool(name="res", bufs=3))
        psum_v = ctx.enter_context(tc.psum_pool(name="psum_v", bufs=PAIR))
        psum_turn = ctx.enter_context(tc.psum_pool(name="psum_turn", bufs=3))
        psum_o = ctx.enter_context(tc.psum_pool(name="psum_o", bufs=N_T))

        pos_rows = const.tile([P, POS_TILES * DIM], BF16)
        nc.sync.dma_start(
            out=pos_rows[:].rearrange("p (b d) -> p b d", b=POS_TILES),
            in_=pos_features.rearrange("(b p) d -> p b d", p=P),
        )
        gen_sb = const.tile([P, TILES * DIM], BF16)
        load_cols = 8 * DIM
        first_cols = FIRST_LOAD * DIM
        nc.sync.dma_start(out=gen_sb[:, 0:first_cols], in_=gen_rows[:, 0:first_cols])
        if first_cols < load_cols:
            nc.sync.dma_start(out=gen_sb[:, first_cols:load_cols], in_=gen_rows[:, first_cols:load_cols])
        pos_k = const.tile([P, PACK * DIM], BF16)
        nc.sync.dma_start(
            out=pos_k[:].rearrange("w (u r) -> w u r", u=2),
            in_=pos_features.rearrange("(u w h) c -> w u (h c)", u=2, h=HALVES),
        )
        scale_bf = const.tile([P, N_T], BF16)
        nc.sync.dma_start(out=scale_bf[:], in_=drift_scales.partition_broadcast(P))
        for c0 in range(load_cols, TILES * DIM, load_cols):
            nc.sync.dma_start(out=gen_sb[:, c0 : c0 + load_cols], in_=gen_rows[:, c0 : c0 + load_cols])
        gen_words = gen_sb[:].bitcast(F32)

        ident = const.tile([P, P], F32)
        make_identity(nc, ident[:])

        warm = const.tile([P, 1], F32)
        nc.vector.memset(warm[:], 1.0)
        nc.scalar.activation(out=warm[:], in_=warm[:], func=FUNC.Sqrt)

        gen_sq = const.tile([P, TILES], F32)
        v_max = const.tile([P, TILES], F32)
        s_min = const.tile([P, TILES], F32)
        d_min = const.tile([P, TILES], F32)
        shift = const.tile([P, N_T * TILES], F32)
        row_sum = const.tile([P, TILES * N_T], F32)
        denom = const.tile([P, TILES * N_T], F32)
        weight = const.tile([P, TILES * N_T], F32)

        pos_sq = const.tile([P, POS_TILES], F32)
        for b in range(POS_TILES):
            squares = junk_pool.tile([P, DIM], BF16)
            nc.scalar.activation(
                out=squares[:],
                in_=pos_rows[:, b * DIM : (b + 1) * DIM],
                func=FUNC.Square,
                accum_out=pos_sq[:, b : b + 1],
            )
        pos_words = pos_rows[:].bitcast(F32)
        idle = const.tile([P, N_POS], BF16)
        nc.vector.memset(idle[:], 0.0)
        idle_ps = psum_o.tile([P, N_POS], F32, tag="prod")

        def keep_warm(count):
            for n in range(count):
                nc.tensor.matmul(idle_ps[:], lhsT=idle[:, 0:P], rhs=idle[:], start=True, stop=True)

        keep_warm(WARM1)
        pos_turned = psum_turn.tile([P, POS_TILES * P], F32, tag="turned")
        for b in range(POS_TILES):
            nc.tensor.transpose(
                pos_turned[:, b * P : (b + 1) * P], pos_words[:, b * WORDS : (b + 1) * WORDS], ident[:]
            )
        pos2_t = const.tile([P, HALVES * N_POS], BF16)
        keep_warm(WARM2)
        pos_halves = pos_turned[:].bitcast(BF16).rearrange("w (j h) -> w h j", h=HALVES)
        for h in range(HALVES):
            pos2_h = pos2_t[:, h * N_POS : (h + 1) * N_POS]
            if h < SPLIT:
                nc.vector.tensor_scalar(out=pos2_h, in0=pos_halves[:, h, :], scalar1=2.0, scalar2=None, op0=ALU.mult)
            else:
                nc.scalar.activation(out=pos2_h, in_=pos_halves[:, h, :], func=FUNC.Copy, scale=2.0)
        neg_pos_sq = const.tile([P, POS_TILES * P], F32)
        nc.vector.tensor_scalar(
            out=neg_pos_sq[:].rearrange("p (b c) -> p b c", b=POS_TILES),
            in0=pos_sq[:].unsqueeze(2).to_broadcast([P, POS_TILES, P]),
            scalar1=-1.0,
            scalar2=None,
            op0=ALU.mult,
        )

        drift = const.tile([P, N_T], F32)
        nc.vector.tensor_copy(out=drift[:], in_=scale_bf[:])

        gen_turned_of = {}
        gen_t_of = {}
        v_of = {}
        dist_of = {}
        e_of = {}
        turned_of = {}
        grouped_of = {}
        codes_of = {}
        scales_of = {}
        prod_of = {}

        def norms(k):
            for a in range(PAIR):
                i = k * PAIR + a
                squares = junk_pool.tile([P, DIM], BF16)
                nc.scalar.activation(
                    out=squares[:],
                    in_=gen_sb[:, i * DIM : (i + 1) * DIM],
                    func=FUNC.Square,
                    accum_out=gen_sq[:, i : i + 1],
                )

        def turn_gen(k):
            gen_turned = psum_turn.tile([P, 2 * PAIR * P], F32, tag="turned")
            for a in range(2 * PAIR):
                i = k * PAIR + a
                nc.tensor.transpose(
                    gen_turned[:, a * P : (a + 1) * P], gen_words[:, i * WORDS : (i + 1) * WORDS], ident[:]
                )
            gen_turned_of[k] = gen_turned

        def empty_gen(k):
            gen_t = gen_t_pool.tile([P, 2 * PAIR * P], F32)
            nc.vector.tensor_copy(out=gen_t[:], in_=gen_turned_of[k][:])
            gen_t_of[k] = gen_t

        def gram(k):
            halves = gen_t_of[k - k % 2][:].bitcast(BF16).rearrange("w (a i h) -> w a i h", a=2 * PAIR, h=HALVES)
            for a in range(PAIR):
                v_ps = psum_v.tile([P, N_POS], F32)
                for b in range(POS_TILES):
                    nc.tensor.matmul(
                        v_ps[:, b * P : (b + 1) * P],
                        lhsT=neg_pos_sq[:, b * P : (b + 1) * P],
                        rhs=ident[:],
                        is_transpose=True,
                        start=(b == 0),
                        stop=False,
                    )
                for h in range(HALVES):
                    nc.tensor.matmul(
                        v_ps[:],
                        lhsT=halves[:, k % 2 * PAIR + a, :, h],
                        rhs=pos2_t[:, h * N_POS : (h + 1) * N_POS],
                        start=False,
                        stop=(h == HALVES - 1),
                    )
                v_of[(k, a)] = v_ps

        def clamp(k):
            dist = dist_pool.tile([P, PAIR, N_POS], F32)
            for a in range(PAIR):
                i = k * PAIR + a
                nc.vector.tensor_scalar(
                    out=dist[:, a, :],
                    in0=v_of[(k, a)][:],
                    scalar1=gen_sq[:, i : i + 1],
                    scalar2=None,
                    op0=ALU.min,
                    op1=ALU.max,
                    accum_out=v_max[:, i : i + 1],
                )
            dist_of[k] = dist
            for first, end in BATCHES:
                if k == end - 1:
                    cols = slice(first * PAIR, end * PAIR)
                    nc.vector.tensor_tensor(
                        out=s_min[:, cols], in0=gen_sq[:, cols], in1=v_max[:, cols], op=ALU.subtract
                    )

        def roots(first, end):
            for k in range(first, end):
                for a in range(PAIR):
                    i = k * PAIR + a
                    nc.scalar.activation(
                        out=dist_of[k][:, a, :],
                        in_=dist_of[k][:, a, :],
                        func=FUNC.Sqrt,
                        scale=-1.0,
                        bias=gen_sq[:, i : i + 1],
                    )
            lo, hi = first * PAIR, end * PAIR
            nc.scalar.activation(out=d_min[:, lo:hi], in_=s_min[:, lo:hi], func=FUNC.Sqrt)
            for t in range(N_T):
                nc.scalar.mul(
                    out=shift[:, t * TILES + lo : t * TILES + hi], in_=d_min[:, lo:hi], mul=1.0 / TEMPS[t]
                )

        def exps(k):
            e_sb = e_pool.tile([P, N_T * PAIR * N_POS], BF16)
            for t in range(N_T):
                for a in range(PAIR):
                    i = k * PAIR + a
                    unit = t * PAIR + a
                    nc.scalar.activation(
                        out=e_sb[:, unit * N_POS : (unit + 1) * N_POS],
                        in_=dist_of[k][:, a, :],
                        func=FUNC.Exp,
                        scale=-1.0 / TEMPS[t],
                        bias=shift[:, t * TILES + i : t * TILES + i + 1],
                        accum_out=row_sum[:, i * N_T + t : i * N_T + t + 1],
                    )
            e_of[k] = e_sb

        def turn(k, t):
            e_words = e_of[k][:].bitcast(F32)
            turned = psum_turn.tile([P, PAIR * 2 * P], F32, tag="turned")
            for q in range(PAIR * 2):
                col = (t * PAIR * 2 + q) * P
                nc.tensor.transpose(turned[:, q * P : (q + 1) * P], e_words[:, col : col + P], ident[:])
            turned_of[(k, t)] = turned

        def empty(k, t):
            if t == 1:
                grouped = grouped_of[(k, 0)]
            elif t == 0:
                grouped = mx_pool.tile([P, 2 * PAIR * N_POS], BF16, align_bytes=64, tag="grouped_two", bufs=2)
            else:
                grouped = mx_pool.tile([P, PAIR * N_POS], BF16, align_bytes=64, tag="grouped_one", bufs=2)
            part = grouped[:, (t % 2) * PAIR * N_POS : (t % 2 + 1) * PAIR * N_POS] if t < 2 else grouped[:]
            on_scalar = (t == 0 and k >= TAIL_E) or (t == 1 and k >= TAIL_E2)
            copy = nc.scalar.copy if on_scalar else nc.vector.tensor_copy
            copy(
                out=part.bitcast(F32).rearrange("w (a i u) -> w a i u", a=PAIR, u=2),
                in_=turned_of[(k, t)][:].rearrange("w (a u i) -> w a i u", a=PAIR, u=2),
            )
            grouped_of[(k, t)] = grouped

        def quantise(k, t):
            width = PAIR * P * (2 if t == 0 else 1)
            codes = mx_pool.tile([P, width], U32, align_bytes=64, tag="codes_%d" % t, bufs=2)
            scales = mx_pool.tile([P, width], U8, align_bytes=64, tag="scales_%d" % t, bufs=2)
            nc.vector.quantize_mx(out=codes[:].bitcast(FP8X4), scales=scales[:], in_=grouped_of[(k, t)][:])
            for n in range(width // (PAIR * P)):
                codes_of[(k, t + n)] = codes[:, n * PAIR * P : (n + 1) * PAIR * P]
                scales_of[(k, t + n)] = scales[:, n * PAIR * P : (n + 1) * PAIR * P]

        pos_codes = const.tile([P, DIM], U32, align_bytes=64)
        pos_scales = const.tile([P, DIM], U8, align_bytes=64)

        def quantise_pos():
            pos_grouped = const.tile([P, DIM * PACK], BF16, align_bytes=64)
            nc.vector.tensor_copy(
                out=pos_grouped[:].rearrange("w (c r) -> w c r", r=PACK),
                in_=pos_k[:].rearrange("w (r c) -> w c r", r=PACK),
            )
            nc.vector.quantize_mx(out=pos_codes[:].bitcast(FP8X4), scales=pos_scales[:], in_=pos_grouped[:])

        def denominators(k):
            cols = slice(k * PAIR * N_T, (k + 2) * PAIR * N_T)
            nc.vector.tensor_tensor(
                out=denom[:, cols].rearrange("p (a t) -> p a t", t=N_T),
                in0=row_sum[:, cols].rearrange("p (a t) -> p a t", t=N_T),
                in1=drift[:].unsqueeze(1).to_broadcast([P, 2 * PAIR, N_T]),
                op=ALU.mult,
            )

        def weights(k):
            cols = slice(k * PAIR * N_T, (k + 2) * PAIR * N_T)
            nc.vector.reciprocal(out=weight[:, cols], in_=denom[:, cols])

        def products(k):
            for t in range(N_T):
                prod = psum_o.tile([P, PAIR * DIM], F32, tag="prod")
                for a in range(PAIR):
                    nc.tensor.matmul_mx(
                        out=prod[:, a * DIM : (a + 1) * DIM],
                        lhsT=codes_of[(k, t)][:, a * P : (a + 1) * P].bitcast(FP8X4),
                        lhsT_scale=scales_of[(k, t)][:, a * P : (a + 1) * P],
                        rhs=pos_codes[:].bitcast(FP8X4),
                        rhs_scale=pos_scales[:],
                        start=True,
                        stop=True,
                    )
                prod_of[(k, t)] = prod

        def combine(k):
            res = res_pool.tile([P, PAIR * DIM], F32)
            for t in range(N_T):
                for a in range(PAIR):
                    i = k * PAIR + a
                    cols = slice(a * DIM, (a + 1) * DIM)
                    w_col = weight[:, i * N_T + t : i * N_T + t + 1]
                    if t == 0 and k >= LAST_TERM:
                        nc.scalar.activation(
                            out=res[:, cols], in_=prod_of[(k, t)][:, cols], func=FUNC.Copy, scale=w_col
                        )
                    elif t == 0:
                        nc.vector.tensor_scalar(
                            out=res[:, cols], in0=prod_of[(k, t)][:, cols], scalar1=w_col, scalar2=None, op0=ALU.mult
                        )
                    else:
                        nc.vector.scalar_tensor_tensor(
                            out=res[:, cols],
                            in0=prod_of[(k, t)][:, cols],
                            scalar=w_col,
                            in1=res[:, cols],
                            op0=ALU.mult,
                            op1=ALU.add,
                        )
            nc.sync.dma_start(out=out_rows[:, k * PAIR * DIM : (k + 1) * PAIR * DIM], in_=res[:])

        def made(k):
            return min(HEAD + PACE * max(k + 1 + LEAD, 0), AHEAD + k + 1, STEPS) if k >= -1 - LEAD else HEAD

        def tick(k):
            new = range(made(k), made(k + 1))
            live = 0 <= k < STEPS
            for j in range(made(k + NLEAD), made(k + NLEAD + 1)):
                norms(j)
            if live:
                empty(k, 0)
                empty(k, 1)
                empty(k, 2)
                quantise(k, 0)
            for far in new:
                if far % 2 == 0 and far + 2 < STEPS:
                    turn_gen(far + 2)
                    empty_gen(far + 2)
                if far == made(k):
                    gram(far)
            if live and k % 2 == 0:
                denominators(k)
            if k >= 1:
                combine(k - 1)
            if live:
                quantise(k, 2)
            for far in new:
                if far > made(k):
                    gram(far)
                clamp(far)
            if live and k % 2 == 0:
                weights(k)
            if 0 <= k + 1 < STEPS:
                for t in range(N_T):
                    turn(k + 1, t)
            if live:
                products(k)

        for k in range(made(-1 - LEAD + NLEAD)):
            norms(k)
        turn_gen(0)
        empty_gen(0)
        for k in range(HEAD):
            if k % 2 == 0:
                turn_gen(k + 2)
                empty_gen(k + 2)
            gram(k)
            clamp(k)
            if k == 1:
                quantise_pos()

        for first, end in BATCHES:
            roots(first, end)
            for s in range(first, end):
                exps(s)
                tick(s - 1 - LEAD)
        for k in range(STEPS - 1 - LEAD, STEPS + 1):
            tick(k)
